import numpy as np
import ml_dtypes


def mxq(x, axis, fmt="e4m3"):
    dtype, down = {"e4m3": (ml_dtypes.float8_e4m3fn, 7), "e5m2": (ml_dtypes.float8_e5m2, 14)}[fmt]
    v = np.moveaxis(np.asarray(x, np.float32).astype(ml_dtypes.bfloat16).astype(np.float64), axis, -1)
    blocks = v.reshape(v.shape[:-1] + (-1, 32))
    amax = np.abs(blocks).max(-1, keepdims=True)
    byte = np.maximum(np.where(amax > 0, np.frexp(amax)[1] - 1 + 127, 0) - down, 1)
    scale = np.exp2(byte - 127.0)
    codes = (blocks / scale).astype(np.float32).astype(dtype).astype(np.float64)
    return np.moveaxis((codes * scale).reshape(v.shape), -1, axis)


WIDE = False


def mx_kscale(k):
    if not WIDE:
        return np.ones(k)
    levels = np.array([10, -10, 5, -5, 0])
    if k % 512:
        return np.exp2(np.random.permutation(np.resize(levels, k // 32))).repeat(32)
    a = np.empty((k // 512, 16))
    for p in range(k // 512):
        a[p, :8] = np.random.permutation(np.resize(levels, 8))
        for g in range(8):
            far = levels[np.abs(levels - a[p, g]) >= 10]
            a[p, g + 8] = far[np.random.randint(len(far))]
    return np.exp2(a.ravel()).repeat(32)


BF16 = ml_dtypes.bfloat16


def bf(x):
    return np.asarray(x, np.float32).astype(BF16)


def f64(x):
    return np.asarray(x).astype(np.float64)


B, T, D, H, NUM_LAYERS = 4, 2048, 512, 512, 3
EPS = 1e-8


def setup_inputs():
    s = mx_kscale(D)
    return {"inv": bf(np.random.standard_normal((B, T, D)) * 0.5 * s),
            "Wk": bf(np.random.standard_normal((D, D)) * 2.0 / np.sqrt(D) / s[None, :]),
            "bk": bf(2.5 / np.sqrt(D) + 0.7 * np.random.standard_normal(D))}


def reference(inv, Wk, bk):
    flat = f64(inv).reshape(-1, D)
    out = (mxq(flat, 1, "e4m3") @ mxq(f64(Wk), 1, "e4m3").T) + f64(bk)
    sqrtD = np.sqrt(D)
    S = out.sum(-1, keepdims=True)
    norms = np.sqrt((out * out).sum(-1, keepdims=True))
    c = out * S / (np.maximum(np.abs(out) * sqrtD, EPS) * np.maximum(norms, EPS))
    diff = np.abs(c[1:] - c[:-1]).sum(0)
    return np.broadcast_to(diff, (D, D)).copy()

@@ -1,0 +1,285 @@
+import math
+from contextlib import ExitStack
+
+import concourse.mybir as mybir
+from concourse.masks import make_identity
+
+FLOPS = 2 * 8192 * 512 * 512
+
+F32 = mybir.dt.float32
+BF16 = mybir.dt.bfloat16
+U32 = mybir.dt.uint32
+U8 = mybir.dt.uint8
+FP8X4 = mybir.dt.float8_e4m3fn_x4
+ALU = mybir.AluOpType
+ACT = mybir.ActivationFunctionType
+AX = mybir.AxisListType
+
+P = 128
+D = 512
+NT = 64
+NG = 16
+EPS = 1e-8
+DELTA = EPS / math.sqrt(D)
+
+
+def tile_dispatcher_pa_kernel(tc, inv, Wk, bk, out):
+    nc = tc.nc
+    rows = inv.flatten_outer_dims().rearrange("(p t) k -> p t k", t=NT)
+    with ExitStack() as ctx:
+        const = ctx.enter_context(tc.tile_pool(name="const", bufs=1))
+        work = ctx.enter_context(tc.tile_pool(name="work", bufs=3))
+        small = ctx.enter_context(tc.tile_pool(name="small", bufs=3))
+        psum = ctx.enter_context(tc.psum_pool(name="psum", bufs=2))
+        ctx.enter_context(tc.manual_schedule())
+
+        b_bf = const.tile([P, D], BF16, name="b_bf")
+        nc.scalar.dma_start(out=b_bf[:], in_=bk.partition_broadcast(P))
+        w_sb = const.tile([P, 4, D], BF16, name="w_sb")
+        w_rows = Wk.rearrange("(a p) k -> p a k", p=P)
+        for h in range(2):
+            nc.sync.dma_start(out=w_sb[:, 2 * h : 2 * h + 2, :], in_=w_rows[:, 2 * h : 2 * h + 2, :])
+        xs = []
+        for g in range(NG):
+            xg = const.tile([P, 4, D], BF16, name="x%d" % g)
+            if g == 0:
+                for h in range(2):
+                    nc.sync.dma_start(out=xg[:, 2 * h : 2 * h + 2, :], in_=rows[:, 2 * h : 2 * h + 2, :])
+            else:
+                nc.sync.dma_start(out=xg[:], in_=rows[:, 4 * g : 4 * g + 4, :])
+            xs.append(xg)
+        one = const.tile([P, 1], F32, name="one")
+        nc.vector.memset(one[:], 1.0)
+        warm = const.tile([P, 1], F32, name="warm")
+        nc.scalar.activation(out=warm[:], in_=one[:], func=ACT.Sqrt)
+        ident = const.tile([P, P], F32, name="ident")
+        make_identity(nc, ident[:])
+        shift = const.tile([P, P], F32, name="shift")
+        nc.vector.tensor_copy(out=shift[:, 1:P], in_=ident[:, 0 : P - 1])
+        nc.vector.tensor_copy(out=shift[:, 0:1], in_=ident[:, P - 1 : P])
+        bias = const.tile([P, D], F32, name="bias")
+        part = const.tile([P, 4, NG + 1], F32, name="part")
+        w_first = const.tile([P, D], F32, name="w_first")
+        w_codes = const.tile([P, D], U32, name="w_codes", align_bytes=64)
+        w_scl = const.tile([P, D], U8, name="w_scl", align_bytes=64)
+        st = {}
+
+        def ok(g):
+            return 0 <= g < NG
+
+        def flip(bank, srcs):
+            for h in range(2):
+                words = srcs[h].bitcast(F32)
+                for u in range(2):
+                    nc.tensor.transpose(bank[:, h, u, :], words[:, u : 2 * P : 2], ident[:])
+
+        def t1(g, h):
+            if ok(g):
+                xt = psum.tile([P, 2, 2, P], F32, tag="xt", name="xt")
+                flip(xt, [xs[g][:, 2 * h, :], xs[g][:, 2 * h + 1, :]])
+                st[("xt", g, h)] = xt
+
+        def cp(g, h):
+            if ok(g):
+                grp = work.tile([P, 2 * D], BF16, tag="grp", name="grp", align_bytes=64)
+                nc.scalar.copy(
+                    out=grp[:].bitcast(F32).rearrange("p (a r u) -> p a r u", a=2, r=P, u=2),
+                    in_=st[("xt", g, h)][:].rearrange("p h u r -> p h r u"),
+                )
+                st[("grp", g, h)] = grp
+
+        def qz(g, h):
+            if ok(g):
+                codes = work.tile([P, 2 * P], U32, tag="codes", name="codes", align_bytes=64)
+                scl = work.tile([P, 2 * P], U8, tag="scl", name="scl", align_bytes=64)
+                nc.vector.quantize_mx(out=codes[:].bitcast(FP8X4), scales=scl[:], in_=st[("grp", g, h)][:])
+                st[("codes", g, h)] = codes
+                st[("scl", g, h)] = scl
+
+        def mx(g, a):
+            if ok(g):
+                acc = psum.tile([P, D], F32, tag="acc", name="acc")
+                c0 = (a % 2) * P
+                nc.tensor.matmul_mx(
+                    out=acc[:],
+                    lhsT=st[("codes", g, a // 2)][:, c0 : c0 + P].bitcast(FP8X4),
+                    lhsT_scale=st[("scl", g, a // 2)][:, c0 : c0 + P],
+                    rhs=w_codes[:].bitcast(FP8X4),
+                    rhs_scale=w_scl[:],
+                    start=True,
+                    stop=True,
+                )
+                st[("acc", g, a)] = acc
+
+        def p1(g, a):
+            if ok(g):
+                if a == 0:
+                    st[("ssum", g)] = small.tile([P, 4], F32, tag="ssum", name="ssum")
+                    st[("n2", g)] = small.tile([P, 4], F32, tag="n2", name="n2")
+                if a % 2 == 0:
+                    st[("o", g, a // 2)] = work.tile([P, 2, D], F32, tag="o", name="o")
+                nc.vector.scalar_tensor_tensor(
+                    out=st[("o", g, a // 2)][:, a % 2, :],
+                    in0=st[("acc", g, a)][:],
+                    scalar=1.0,
+                    in1=bias[:],
+                    op0=ALU.mult,
+                    op1=ALU.add,
+                    accum_out=st[("ssum", g)][:, a : a + 1],
+                )
+
+        def p2(g, a):
+            if ok(g):
+                junk = work.tile([P, D], F32, tag="junk", name="junk")
+                nc.scalar.activation(
+                    out=junk[:],
+                    in_=st[("o", g, a // 2)][:, a % 2, :],
+                    func=ACT.Square,
+                    accum_out=st[("n2", g)][:, a : a + 1],
+                )
+
+        def tau(g, h):
+            if ok(g):
+                tt = work.tile([P, 2, D], F32, tag="tau", name="tt", bufs=4)
+                nc.vector.tensor_scalar(
+                    out=tt[:], in0=st[("o", g, h)][:], scalar1=DELTA, scalar2=-DELTA, op0=ALU.min, op1=ALU.max
+                )
+                st[("tau", g, h)] = tt
+
+        def m2(g):
+            if ok(g):
+                mm = small.tile([P, 4], F32, tag="m2", name="mm")
+                nc.vector.tensor_scalar(
+                    out=mm[:], in0=st[("n2", g)][:], scalar1=EPS * EPS, scalar2=None, op0=ALU.max
+                )
+                st[("m2", g)] = mm
+
+        def root(g):
+            if ok(g):
+                nn = small.tile([P, 4], F32, tag="nn", name="nn")
+                nc.scalar.activation(out=nn[:], in_=st[("m2", g)][:], func=ACT.Sqrt)
+                st[("nn", g)] = nn
+
+        def rec(g):
+            if ok(g):
+                rc = small.tile([P, 4], F32, tag="rc", name="rc")
+                nc.vector.reciprocal(out=rc[:], in_=st[("nn", g)][:])
+                r2 = small.tile([P, 4], F32, tag="r2", name="r2")
+                nc.vector.scalar_tensor_tensor(
+                    out=r2[:], in0=st[("ssum", g)][:], scalar=1.0 / EPS, in1=rc[:], op0=ALU.mult, op1=ALU.mult
+                )
+                st[("r2", g)] = r2
+
+        def wt(g, a):
+            if ok(g):
+                if g == 0 and a == 0:
+                    ww = w_first
+                else:
+                    ww = work.tile([P, D], F32, tag="w", name="ww", bufs=12)
+                nc.vector.tensor_scalar(
+                    out=ww[:],
+                    in0=st[("tau", g, a // 2)][:, a % 2, :],
+                    scalar1=st[("r2", g)][:, a : a + 1],
+                    scalar2=(1.0 if a % 2 == 0 else -1.0),
+                    op0=ALU.mult,
+                    op1=ALU.mult,
+                )
+                st[("w", 4 * g + a)] = ww
+
+        def add_flipped(dst, first, second, perm, j, plain):
+            nc.tensor.matmul(
+                out=dst,
+                lhsT=first[:, j * P : (j + 1) * P],
+                rhs=ident[:],
+                is_transpose=(not plain),
+                start=True,
+                stop=False,
+            )
+            nc.tensor.matmul(
+                out=dst, lhsT=second[:, j * P : (j + 1) * P], rhs=perm[:], is_transpose=True, start=False, stop=True
+            )
+
+        def ed(g, j):
+            if 0 <= g <= NG:
+                eb = psum.tile([P, 4, P], F32, tag="e%d" % j, name="eb", bufs=1)
+                if g == NG:
+                    add_flipped(eb[:, 0, :], st[("w", 0)], st[("w", NT - 1)], shift, j, False)
+                else:
+                    for q in range(4):
+                        if 4 * g + q >= 1:
+                            add_flipped(
+                                eb[:, q, :], st[("w", 4 * g + q - 1)], st[("w", 4 * g + q)], ident, j, q == 1
+                            )
+                st[("e", g, j)] = eb
+
+        def ab(g, j):
+            if 0 <= g <= NG:
+                flat = st[("e", g, j)][:].rearrange("p q r -> p (q r)")
+                lo, hi = 0, D
+                if g == 0:
+                    lo = P
+                if g == NG:
+                    lo, hi = 1, P
+                junk = work.tile([P, D], F32, tag="junk", name="junk")
+                nc.scalar.activation(
+                    out=junk[:, lo:hi], in_=flat[:, lo:hi], func=ACT.Abs, accum_out=part[:, j, g : g + 1]
+                )
+
+        grp_w = const.tile([P, 4 * D], BF16, name="grp_w", align_bytes=64)
+        for h in range(2):
+            wb = psum.tile([P, 2, 2, P], F32, tag="e%d" % h, name="wb", bufs=1)
+            flip(wb, [w_sb[:, 2 * h, :], w_sb[:, 2 * h + 1, :]])
+            nc.vector.tensor_copy(
+                out=grp_w[:, 2 * h * D : (2 * h + 2) * D].bitcast(F32).rearrange("p (a r u) -> p a r u", a=2, r=P, u=2),
+                in_=wb[:].rearrange("p h u r -> p h r u"),
+            )
+        nc.vector.quantize_mx(out=w_codes[:].bitcast(FP8X4), scales=w_scl[:], in_=grp_w[:])
+        nc.vector.tensor_copy(out=bias[:], in_=b_bf[:])
+
+        for i in range(-2, NG + 4):
+            ed(i - 2, 0)
+            ab(i - 3, 3)
+            p1(i, 0)
+            m2(i - 1)
+            mx(i, 2)
+            p2(i, 0)
+            root(i - 1)
+            qz(i + 1, 0)
+            ed(i - 2, 1)
+            t1(i + 1, 1)
+            ab(i - 2, 0)
+            p1(i, 1)
+            mx(i, 3)
+            p2(i, 1)
+            tau(i, 0)
+            rec(i - 1)
+            cp(i + 1, 1)
+            ed(i - 2, 2)
+            t1(i + 2, 0)
+            ab(i - 2, 1)
+            p1(i, 2)
+            p2(i, 2)
+            wt(i - 1, 0)
+            wt(i - 1, 1)
+            cp(i + 2, 0)
+            ed(i - 2, 3)
+            p1(i, 3)
+            mx(i + 1, 0)
+            mx(i + 1, 1)
+            p2(i, 3)
+            ab(i - 2, 2)
+            wt(i - 1, 2)
+            wt(i - 1, 3)
+            tau(i, 1)
+            qz(i + 1, 1)
+
+        dcol = small.tile([P, 4], F32, tag="dcol", name="dcol")
+        nc.vector.tensor_reduce(out=dcol[:], in_=part[:], axis=AX.X, op=ALU.add)
+        fin = psum.tile([P, D], F32, tag="acc", name="fin")
+        for j in range(4):
+            nc.tensor.transpose(fin[:, j * P : (j + 1) * P], dcol[:, j : j + 1].to_broadcast([P, P]), ident[:])
+        res = const.tile([P, D], F32, name="res")
+        nc.vector.tensor_copy(out=res[:], in_=fin[:])
+        for a in range(4):
+            eng = nc.sync if a % 2 == 0 else nc.scalar
+            eng.dma_start(out=out[a * P : (a + 1) * P, :], in_=res[:])

@@ -98,7 +98,7 @@ def tile_dispatcher_pa_kernel(tc, inv, Wk, bk, out):
 
         def mx(g, a):
             if ok(g):
-                acc = psum.tile([P, D], F32, tag="acc", name="acc")
+                acc = psum.tile([P, D], F32, tag="acc", name="acc", bufs=4)
                 c0 = (a % 2) * P
                 nc.tensor.matmul_mx(
                     out=acc[:],
@@ -201,7 +201,7 @@ def tile_dispatcher_pa_kernel(tc, inv, Wk, bk, out):
 
         def ed(g, j):
             if 0 <= g <= NG:
-                eb = psum.tile([P, 4, P], F32, tag="e%d" % j, name="eb", bufs=1)
+                eb = psum.tile([P, 4, P], F32, tag="e", name="eb")
                 if g == NG:
                     add_flipped(eb[:, 0, :], st[("w", 0)], st[("w", NT - 1)], shift, j, False)
                 else:
@@ -227,7 +227,7 @@ def tile_dispatcher_pa_kernel(tc, inv, Wk, bk, out):
 
         grp_w = const.tile([P, 4 * D], BF16, name="grp_w", align_bytes=64)
         for h in range(2):
-            wb = psum.tile([P, 2, 2, P], F32, tag="e%d" % h, name="wb", bufs=1)
+            wb = psum.tile([P, 2, 2, P], F32, tag="e", name="wb")
             flip(wb, [w_sb[:, 2 * h, :], w_sb[:, 2 * h + 1, :]])
             nc.vector.tensor_copy(
                 out=grp_w[:, 2 * h * D : (2 * h + 2) * D].bitcast(F32).rearrange("p (a r u) -> p a r u", a=2, r=P, u=2),
@@ -239,43 +239,41 @@ def tile_dispatcher_pa_kernel(tc, inv, Wk, bk, out):
         for i in range(-2, NG + 4):
             ed(i - 2, 0)
             ab(i - 3, 3)
-            p1(i, 0)
             m2(i - 1)
-            mx(i, 2)
-            p2(i, 0)
+            p1(i, 0)
             root(i - 1)
-            qz(i + 1, 0)
+            p2(i, 0)
             ed(i - 2, 1)
-            t1(i + 1, 1)
             ab(i - 2, 0)
             p1(i, 1)
-            mx(i, 3)
-            p2(i, 1)
-            tau(i, 0)
             rec(i - 1)
-            cp(i + 1, 1)
-            ed(i - 2, 2)
+            p2(i, 1)
             t1(i + 2, 0)
             ab(i - 2, 1)
-            p1(i, 2)
-            p2(i, 2)
+            qz(i + 1, 0)
             wt(i - 1, 0)
             wt(i - 1, 1)
+            p1(i, 2)
+            ed(i - 2, 2)
             cp(i + 2, 0)
-            ed(i - 2, 3)
+            p2(i, 2)
+            tau(i, 0)
+            qz(i + 1, 1)
             p1(i, 3)
-            mx(i + 1, 0)
-            mx(i + 1, 1)
-            p2(i, 3)
+            ed(i - 2, 3)
             ab(i - 2, 2)
+            p2(i, 3)
+            t1(i + 2, 1)
+            cp(i + 2, 1)
             wt(i - 1, 2)
             wt(i - 1, 3)
             tau(i, 1)
-            qz(i + 1, 1)
+            for a in range(4):
+                mx(i + 1, a)
 
         dcol = small.tile([P, 4], F32, tag="dcol", name="dcol")
         nc.vector.tensor_reduce(out=dcol[:], in_=part[:], axis=AX.X, op=ALU.add)
-        fin = psum.tile([P, D], F32, tag="acc", name="fin")
+        fin = psum.tile([P, D], F32, tag="acc", name="fin", bufs=4)
         for j in range(4):
             nc.tensor.transpose(fin[:, j * P : (j + 1) * P], dcol[:, j : j + 1].to_broadcast([P, P]), ident[:])
         res = const.tile([P, D], F32, name="res")

@@ -51,12 +51,17 @@ def tile_dispatcher_pa_kernel(tc, inv, Wk, bk, out):
         one = const.tile([P, 1], F32, name="one")
         nc.vector.memset(one[:], 1.0)
         warm = const.tile([P, 1], F32, name="warm")
-        nc.scalar.activation(out=warm[:], in_=one[:], func=ACT.Sqrt)
+        nc.scalar.activation(out=warm[:], in_=one[:], func=ACT.Abs_reciprocal_sqrt)
         ident = const.tile([P, P], F32, name="ident")
         make_identity(nc, ident[:])
         shift = const.tile([P, P], F32, name="shift")
         nc.vector.tensor_copy(out=shift[:, 1:P], in_=ident[:, 0 : P - 1])
         nc.vector.tensor_copy(out=shift[:, 0:1], in_=ident[:, P - 1 : P])
+        turn = const.tile([P, 4], F32, name="turn")
+        for a in range(4):
+            nc.vector.tensor_scalar(
+                out=turn[:, a : a + 1], in0=one[:], scalar1=(1.0 if a % 2 == 0 else -1.0) / EPS, scalar2=None, op0=ALU.mult
+            )
         bias = const.tile([P, D], F32, name="bias")
         part = const.tile([P, 4, NG + 1], F32, name="part")
         w_first = const.tile([P, D], F32, name="w_first")
@@ -81,29 +86,30 @@ def tile_dispatcher_pa_kernel(tc, inv, Wk, bk, out):
 
         def cp(g, h):
             if ok(g):
-                grp = work.tile([P, 2 * D], BF16, tag="grp", name="grp", align_bytes=64)
-                nc.scalar.copy(
-                    out=grp[:].bitcast(F32).rearrange("p (a r u) -> p a r u", a=2, r=P, u=2),
+                if h == 0:
+                    st[("grp", g)] = work.tile([P, 4 * D], BF16, tag="grp", name="grp", align_bytes=64)
+                grp = st[("grp", g)][:, 2 * h * D : (2 * h + 2) * D]
+                (nc.vector.tensor_copy)(
+                    out=grp.bitcast(F32).rearrange("p (a r u) -> p a r u", a=2, r=P, u=2),
                     in_=st[("xt", g, h)][:].rearrange("p h u r -> p h r u"),
                 )
-                st[("grp", g, h)] = grp
 
-        def qz(g, h):
+        def qz(g):
             if ok(g):
-                codes = work.tile([P, 2 * P], U32, tag="codes", name="codes", align_bytes=64)
-                scl = work.tile([P, 2 * P], U8, tag="scl", name="scl", align_bytes=64)
-                nc.vector.quantize_mx(out=codes[:].bitcast(FP8X4), scales=scl[:], in_=st[("grp", g, h)][:])
-                st[("codes", g, h)] = codes
-                st[("scl", g, h)] = scl
+                codes = work.tile([P, 4 * P], U32, tag="codes", name="codes", align_bytes=64)
+                scl = work.tile([P, 4 * P], U8, tag="scl", name="scl", align_bytes=64)
+                nc.vector.quantize_mx(out=codes[:].bitcast(FP8X4), scales=scl[:], in_=st[("grp", g)][:])
+                st[("codes", g)] = codes
+                st[("scl", g)] = scl
 
         def mx(g, a):
             if ok(g):
                 acc = psum.tile([P, D], F32, tag="acc", name="acc", bufs=4)
-                c0 = (a % 2) * P
+                c0 = a * P
                 nc.tensor.matmul_mx(
                     out=acc[:],
-                    lhsT=st[("codes", g, a // 2)][:, c0 : c0 + P].bitcast(FP8X4),
-                    lhsT_scale=st[("scl", g, a // 2)][:, c0 : c0 + P],
+                    lhsT=st[("codes", g)][:, c0 : c0 + P].bitcast(FP8X4),
+                    lhsT_scale=st[("scl", g)][:, c0 : c0 + P],
                     rhs=w_codes[:].bitcast(FP8X4),
                     rhs_scale=w_scl[:],
                     start=True,
@@ -116,10 +122,9 @@ def tile_dispatcher_pa_kernel(tc, inv, Wk, bk, out):
                 if a == 0:
                     st[("ssum", g)] = small.tile([P, 4], F32, tag="ssum", name="ssum")
                     st[("n2", g)] = small.tile([P, 4], F32, tag="n2", name="n2")
-                if a % 2 == 0:
-                    st[("o", g, a // 2)] = work.tile([P, 2, D], F32, tag="o", name="o")
+                    st[("o", g)] = work.tile([P, 4, D], F32, tag="o", name="o")
                 nc.vector.scalar_tensor_tensor(
-                    out=st[("o", g, a // 2)][:, a % 2, :],
+                    out=st[("o", g)][:, a, :],
                     in0=st[("acc", g, a)][:],
                     scalar=1.0,
                     in1=bias[:],
@@ -133,40 +138,36 @@ def tile_dispatcher_pa_kernel(tc, inv, Wk, bk, out):
                 junk = work.tile([P, D], F32, tag="junk", name="junk")
                 nc.scalar.activation(
                     out=junk[:],
-                    in_=st[("o", g, a // 2)][:, a % 2, :],
+                    in_=st[("o", g)][:, a, :],
                     func=ACT.Square,
                     accum_out=st[("n2", g)][:, a : a + 1],
                 )
 
-        def tau(g, h):
+        def tau(g):
             if ok(g):
-                tt = work.tile([P, 2, D], F32, tag="tau", name="tt", bufs=4)
+                tt = work.tile([P, 4, D], F32, tag="tau", name="tt")
                 nc.vector.tensor_scalar(
-                    out=tt[:], in0=st[("o", g, h)][:], scalar1=DELTA, scalar2=-DELTA, op0=ALU.min, op1=ALU.max
+                    out=tt[:], in0=st[("o", g)][:], scalar1=DELTA, scalar2=-DELTA, op0=ALU.min, op1=ALU.max
                 )
-                st[("tau", g, h)] = tt
-
-        def m2(g):
-            if ok(g):
-                mm = small.tile([P, 4], F32, tag="m2", name="mm")
-                nc.vector.tensor_scalar(
-                    out=mm[:], in0=st[("n2", g)][:], scalar1=EPS * EPS, scalar2=None, op0=ALU.max
-                )
-                st[("m2", g)] = mm
+                st[("tau", g)] = tt
 
         def root(g):
             if ok(g):
-                nn = small.tile([P, 4], F32, tag="nn", name="nn")
-                nc.scalar.activation(out=nn[:], in_=st[("m2", g)][:], func=ACT.Sqrt)
-                st[("nn", g)] = nn
+                rn = small.tile([P, 4], F32, tag="rn", name="rn")
+                nc.scalar.activation(out=rn[:], in_=st[("n2", g)][:], func=ACT.Abs_reciprocal_sqrt, bias=1e-30)
+                st[("rn", g)] = rn
+
+        def sg(g):
+            if ok(g):
+                sx = small.tile([P, 4], F32, tag="sx", name="sx")
+                nc.gpsimd.tensor_tensor(out=sx[:], in0=st[("ssum", g)][:], in1=turn[:], op=ALU.mult)
+                st[("sx", g)] = sx
 
         def rec(g):
             if ok(g):
-                rc = small.tile([P, 4], F32, tag="rc", name="rc")
-                nc.vector.reciprocal(out=rc[:], in_=st[("nn", g)][:])
                 r2 = small.tile([P, 4], F32, tag="r2", name="r2")
                 nc.vector.scalar_tensor_tensor(
-                    out=r2[:], in0=st[("ssum", g)][:], scalar=1.0 / EPS, in1=rc[:], op0=ALU.mult, op1=ALU.mult
+                    out=r2[:], in0=st[("rn", g)][:], scalar=1.0 / EPS, in1=st[("sx", g)][:], op0=ALU.min, op1=ALU.mult
                 )
                 st[("r2", g)] = r2
 
@@ -176,13 +177,13 @@ def tile_dispatcher_pa_kernel(tc, inv, Wk, bk, out):
                     ww = w_first
                 else:
                     ww = work.tile([P, D], F32, tag="w", name="ww", bufs=12)
-                nc.vector.tensor_scalar(
+                nc.gpsimd.tensor_scalar(
                     out=ww[:],
-                    in0=st[("tau", g, a // 2)][:, a % 2, :],
+                    in0=st[("tau", g)][:, a, :],
                     scalar1=st[("r2", g)][:, a : a + 1],
-                    scalar2=(1.0 if a % 2 == 0 else -1.0),
+                    scalar2=0.0,
                     op0=ALU.mult,
-                    op1=ALU.mult,
+                    op1=ALU.add,
                 )
                 st[("w", 4 * g + a)] = ww
 
@@ -208,7 +209,7 @@ def tile_dispatcher_pa_kernel(tc, inv, Wk, bk, out):
                     for q in range(4):
                         if 4 * g + q >= 1:
                             add_flipped(
-                                eb[:, q, :], st[("w", 4 * g + q - 1)], st[("w", 4 * g + q)], ident, j, q == 1
+                                eb[:, q, :], st[("w", 4 * g + q - 1)], st[("w", 4 * g + q)], ident, j, q == 1 and j in (0, 2)
                             )
                 st[("e", g, j)] = eb
 
@@ -237,39 +238,37 @@ def tile_dispatcher_pa_kernel(tc, inv, Wk, bk, out):
         nc.vector.tensor_copy(out=bias[:], in_=b_bf[:])
 
         for i in range(-2, NG + 4):
-            ed(i - 2, 0)
-            ab(i - 3, 3)
-            m2(i - 1)
-            p1(i, 0)
-            root(i - 1)
-            p2(i, 0)
-            ed(i - 2, 1)
-            ab(i - 2, 0)
-            p1(i, 1)
-            rec(i - 1)
-            p2(i, 1)
-            t1(i + 2, 0)
             ab(i - 2, 1)
-            qz(i + 1, 0)
-            wt(i - 1, 0)
-            wt(i - 1, 1)
-            p1(i, 2)
             ed(i - 2, 2)
-            cp(i + 2, 0)
-            p2(i, 2)
-            tau(i, 0)
-            qz(i + 1, 1)
-            p1(i, 3)
+            p1(i, 0)
+            p2(i, 0)
             ed(i - 2, 3)
             ab(i - 2, 2)
-            p2(i, 3)
+            wt(i - 1, 0)
+            p1(i, 1)
+            p2(i, 1)
+            t1(i + 2, 0)
+            wt(i - 1, 1)
+            p1(i, 2)
+            p2(i, 2)
             t1(i + 2, 1)
-            cp(i + 2, 1)
             wt(i - 1, 2)
+            p1(i, 3)
+            p2(i, 3)
             wt(i - 1, 3)
-            tau(i, 1)
+            sg(i)
+            ab(i - 2, 3)
+            root(i)
+            cp(i + 2, 0)
+            cp(i + 2, 1)
             for a in range(4):
                 mx(i + 1, a)
+            tau(i)
+            ed(i - 1, 0)
+            ab(i - 1, 0)
+            qz(i + 2)
+            rec(i)
+            ed(i - 1, 1)
 
         dcol = small.tile([P, 4], F32, tag="dcol", name="dcol")
         nc.vector.tensor_reduce(out=dcol[:], in_=part[:], axis=AX.X, op=ALU.add)

@@ -63,7 +63,7 @@ def tile_dispatcher_pa_kernel(tc, inv, Wk, bk, out):
                 out=turn[:, a : a + 1], in0=one[:], scalar1=(1.0 if a % 2 == 0 else -1.0) / EPS, scalar2=None, op0=ALU.mult
             )
         bias = const.tile([P, D], F32, name="bias")
-        part = const.tile([P, 4, NG + 1], F32, name="part")
+        part = const.tile([P, NG + 1, 4], F32, name="part")
         w_first = const.tile([P, D], F32, name="w_first")
         w_codes = const.tile([P, D], U32, name="w_codes", align_bytes=64)
         w_scl = const.tile([P, D], U8, name="w_scl", align_bytes=64)
@@ -89,7 +89,8 @@ def tile_dispatcher_pa_kernel(tc, inv, Wk, bk, out):
                 if h == 0:
                     st[("grp", g)] = work.tile([P, 4 * D], BF16, tag="grp", name="grp", align_bytes=64)
                 grp = st[("grp", g)][:, 2 * h * D : (2 * h + 2) * D]
-                (nc.vector.tensor_copy)(
+                move = nc.scalar.copy if g < 3 else nc.vector.tensor_copy
+                move(
                     out=grp.bitcast(F32).rearrange("p (a r u) -> p a r u", a=2, r=P, u=2),
                     in_=st[("xt", g, h)][:].rearrange("p h u r -> p h r u"),
                 )
@@ -105,11 +106,10 @@ def tile_dispatcher_pa_kernel(tc, inv, Wk, bk, out):
         def mx(g, a):
             if ok(g):
                 acc = psum.tile([P, D], F32, tag="acc", name="acc", bufs=4)
-                c0 = a * P
                 nc.tensor.matmul_mx(
                     out=acc[:],
-                    lhsT=st[("codes", g)][:, c0 : c0 + P].bitcast(FP8X4),
-                    lhsT_scale=st[("scl", g)][:, c0 : c0 + P],
+                    lhsT=st[("codes", g)][:, a * P : (a + 1) * P].bitcast(FP8X4),
+                    lhsT_scale=st[("scl", g)][:, a * P : (a + 1) * P],
                     rhs=w_codes[:].bitcast(FP8X4),
                     rhs_scale=w_scl[:],
                     start=True,
@@ -171,13 +171,13 @@ def tile_dispatcher_pa_kernel(tc, inv, Wk, bk, out):
                 )
                 st[("r2", g)] = r2
 
-        def wt(g, a):
+        def wt(g, a, eng):
             if ok(g):
                 if g == 0 and a == 0:
                     ww = w_first
                 else:
                     ww = work.tile([P, D], F32, tag="w", name="ww", bufs=12)
-                nc.gpsimd.tensor_scalar(
+                eng.tensor_scalar(
                     out=ww[:],
                     in0=st[("tau", g)][:, a, :],
                     scalar1=st[("r2", g)][:, a : a + 1],
@@ -186,6 +186,12 @@ def tile_dispatcher_pa_kernel(tc, inv, Wk, bk, out):
                     op1=ALU.add,
                 )
                 st[("w", 4 * g + a)] = ww
+
+        def wg(g, a):
+            wt(g, a, nc.gpsimd)
+
+        def wv(g, a):
+            wt(g, a, nc.vector)
 
         def add_flipped(dst, first, second, perm, j, plain):
             nc.tensor.matmul(
@@ -201,30 +207,57 @@ def tile_dispatcher_pa_kernel(tc, inv, Wk, bk, out):
             )
 
         def ed(g, j):
-            if 0 <= g <= NG:
-                eb = psum.tile([P, 4, P], F32, tag="e", name="eb")
-                if g == NG:
-                    add_flipped(eb[:, 0, :], st[("w", 0)], st[("w", NT - 1)], shift, j, False)
+            if ok(g):
+                if g == NG - 1:
+                    eb = psum.tile([P, 4, P], F32, tag="acc", name="eb", bufs=4)
                 else:
-                    for q in range(4):
-                        if 4 * g + q >= 1:
-                            add_flipped(
-                                eb[:, q, :], st[("w", 4 * g + q - 1)], st[("w", 4 * g + q)], ident, j, q == 1 and j in (0, 2)
-                            )
+                    eb = psum.tile([P, 4, P], F32, tag="e", name="eb")
+                for q in range(4):
+                    if 4 * g + q >= 1:
+                        add_flipped(eb[:, q, :], st[("w", 4 * g + q - 1)], st[("w", 4 * g + q)], ident, j, q == 1)
                 st[("e", g, j)] = eb
 
         def ab(g, j):
-            if 0 <= g <= NG:
+            if ok(g):
                 flat = st[("e", g, j)][:].rearrange("p q r -> p (q r)")
-                lo, hi = 0, D
-                if g == 0:
-                    lo = P
-                if g == NG:
-                    lo, hi = 1, P
+                lo = P if g == 0 else 0
                 junk = work.tile([P, D], F32, tag="junk", name="junk")
                 nc.scalar.activation(
-                    out=junk[:, lo:hi], in_=flat[:, lo:hi], func=ACT.Abs, accum_out=part[:, j, g : g + 1]
+                    out=junk[:, lo:D], in_=flat[:, lo:D], func=ACT.Abs, accum_out=part[:, g, j : j + 1]
                 )
+
+        def pull(g, j):
+            if ok(g):
+                keep = work.tile([P, D], F32, tag="keep", name="keep")
+                nc.vector.tensor_copy(out=keep[:], in_=st[("e", g, j)][:].rearrange("p q r -> p (q r)"))
+                st[("keep", g, j)] = keep
+
+        def av(g, j):
+            if ok(g):
+                nc.vector.tensor_reduce(
+                    out=part[:, g, j : j + 1],
+                    in_=st[("keep", g, j)][:],
+                    axis=AX.X,
+                    op=ALU.add,
+                    apply_absolute_value=True,
+                )
+
+        def seam_edges():
+            eb = psum.tile([P, 4, P], F32, tag="xt", name="eb")
+            for j in range(4):
+                add_flipped(eb[:, j, :], st[("w", 0)], st[("w", NT - 1)], shift, j, False)
+            st["seam"] = eb
+
+        def seam_pull():
+            keep = work.tile([P, 4, P], F32, tag="keep", name="keep")
+            nc.vector.tensor_copy(out=keep[:], in_=st["seam"][:])
+            st["keep"] = keep
+            nc.vector.memset(keep[:, :, 0:1], 0.0)
+
+        def seam_sum():
+            nc.vector.tensor_reduce(
+                out=part[:, NG, :], in_=st["keep"][:], axis=AX.X, op=ALU.add, apply_absolute_value=True
+            )
 
         grp_w = const.tile([P, 4 * D], BF16, name="grp_w", align_bytes=64)
         for h in range(2):
@@ -237,26 +270,26 @@ def tile_dispatcher_pa_kernel(tc, inv, Wk, bk, out):
         nc.vector.quantize_mx(out=w_codes[:].bitcast(FP8X4), scales=w_scl[:], in_=grp_w[:])
         nc.vector.tensor_copy(out=bias[:], in_=b_bf[:])
 
-        for i in range(-2, NG + 4):
+        for i in range(-2, NG):
             ab(i - 2, 1)
             ed(i - 2, 2)
             p1(i, 0)
             p2(i, 0)
-            ed(i - 2, 3)
+            t1(i + 2, 0)
             ab(i - 2, 2)
-            wt(i - 1, 0)
+            wg(i - 1, 0)
             p1(i, 1)
             p2(i, 1)
-            t1(i + 2, 0)
-            wt(i - 1, 1)
+            ed(i - 2, 3)
+            wg(i - 1, 1)
             p1(i, 2)
             p2(i, 2)
             t1(i + 2, 1)
-            wt(i - 1, 2)
+            wg(i - 1, 2)
             p1(i, 3)
             p2(i, 3)
-            wt(i - 1, 3)
             sg(i)
+            wg(i - 1, 3)
             ab(i - 2, 3)
             root(i)
             cp(i + 2, 0)
@@ -269,10 +302,31 @@ def tile_dispatcher_pa_kernel(tc, inv, Wk, bk, out):
             qz(i + 2)
             rec(i)
             ed(i - 1, 1)
+        ab(NG - 2, 1)
+        ed(NG - 2, 2)
+        wg(NG - 1, 0)
+        wv(NG - 1, 1)
+        wv(NG - 1, 2)
+        wv(NG - 1, 3)
+        ed(NG - 2, 3)
+        ab(NG - 2, 2)
+        pull(NG - 2, 3)
+        for j in range(4):
+            ed(NG - 1, j)
+        seam_edges()
+        ab(NG - 1, 0)
+        pull(NG - 1, 1)
+        av(NG - 2, 3)
+        ab(NG - 1, 2)
+        pull(NG - 1, 3)
+        av(NG - 1, 1)
+        seam_pull()
+        av(NG - 1, 3)
+        seam_sum()
 
         dcol = small.tile([P, 4], F32, tag="dcol", name="dcol")
-        nc.vector.tensor_reduce(out=dcol[:], in_=part[:], axis=AX.X, op=ALU.add)
-        fin = psum.tile([P, D], F32, tag="acc", name="fin", bufs=4)
+        nc.vector.tensor_reduce(out=dcol[:], in_=part[:].rearrange("p g j -> p j g"), axis=AX.X, op=ALU.add)
+        fin = psum.tile([P, D], F32, tag="xt", name="fin")
         for j in range(4):
             nc.tensor.transpose(fin[:, j * P : (j + 1) * P], dcol[:, j : j + 1].to_broadcast([P, P]), ident[:])
         res = const.tile([P, D], F32, name="res")

@@ -117,6 +117,18 @@ def tile_dispatcher_pa_kernel(tc, inv, Wk, bk, out):
                 )
                 st[("acc", g, a)] = acc
 
+        def stir(g):
+            acc = psum.tile([P, D], F32, tag="acc", name="acc", bufs=4)
+            nc.tensor.matmul_mx(
+                out=acc[:],
+                lhsT=st[("codes", g)][:, 0:P].bitcast(FP8X4),
+                lhsT_scale=st[("scl", g)][:, 0:P],
+                rhs=w_codes[:].bitcast(FP8X4),
+                rhs_scale=w_scl[:],
+                start=True,
+                stop=True,
+            )
+
         def p1(g, a):
             if ok(g):
                 if a == 0:
@@ -210,11 +222,13 @@ def tile_dispatcher_pa_kernel(tc, inv, Wk, bk, out):
             if ok(g):
                 if g == NG - 1:
                     eb = psum.tile([P, 4, P], F32, tag="acc", name="eb", bufs=4)
+                elif g == NG - 2 and j >= 2:
+                    eb = psum.tile([P, 4, P], F32, tag="xt", name="eb")
                 else:
                     eb = psum.tile([P, 4, P], F32, tag="e", name="eb")
                 for q in range(4):
                     if 4 * g + q >= 1:
-                        add_flipped(eb[:, q, :], st[("w", 4 * g + q - 1)], st[("w", 4 * g + q)], ident, j, q == 1)
+                        add_flipped(eb[:, q, :], st[("w", 4 * g + q - 1)], st[("w", 4 * g + q)], ident, j, q == 1 and j in (1, 3))
                 st[("e", g, j)] = eb
 
         def ab(g, j):
@@ -243,7 +257,7 @@ def tile_dispatcher_pa_kernel(tc, inv, Wk, bk, out):
                 )
 
         def seam_edges():
-            eb = psum.tile([P, 4, P], F32, tag="xt", name="eb")
+            eb = psum.tile([P, 4, P], F32, tag="e", name="eb")
             for j in range(4):
                 add_flipped(eb[:, j, :], st[("w", 0)], st[("w", NT - 1)], shift, j, False)
             st["seam"] = eb
@@ -259,6 +273,9 @@ def tile_dispatcher_pa_kernel(tc, inv, Wk, bk, out):
                 out=part[:, NG, :], in_=st["keep"][:], axis=AX.X, op=ALU.add, apply_absolute_value=True
             )
 
+        hot = psum.tile([P, 2, 2, P], F32, tag="xt", name="hot")
+        for n in range(6):
+            nc.tensor.matmul(out=hot[:, 0, 0, :], lhsT=ident[:], rhs=ident[:], start=True, stop=True)
         grp_w = const.tile([P, 4 * D], BF16, name="grp_w", align_bytes=64)
         for h in range(2):
             wb = psum.tile([P, 2, 2, P], F32, tag="e", name="wb")
@@ -270,59 +287,85 @@ def tile_dispatcher_pa_kernel(tc, inv, Wk, bk, out):
         nc.vector.quantize_mx(out=w_codes[:].bitcast(FP8X4), scales=w_scl[:], in_=grp_w[:])
         nc.vector.tensor_copy(out=bias[:], in_=b_bf[:])
 
-        for i in range(-2, NG):
-            ab(i - 2, 1)
-            ed(i - 2, 2)
+        for i in range(-3, NG - 1):
+            ab(i - 2, 0)
             p1(i, 0)
             p2(i, 0)
-            t1(i + 2, 0)
-            ab(i - 2, 2)
             wg(i - 1, 0)
             p1(i, 1)
             p2(i, 1)
-            ed(i - 2, 3)
+            mx(i + 1, 0)
+            mx(i + 1, 1)
             wg(i - 1, 1)
+            ab(i - 2, 1)
             p1(i, 2)
             p2(i, 2)
-            t1(i + 2, 1)
+            ed(i - 2, 2)
             wg(i - 1, 2)
             p1(i, 3)
             p2(i, 3)
             sg(i)
             wg(i - 1, 3)
-            ab(i - 2, 3)
-            root(i)
             cp(i + 2, 0)
+            t1(i + 3, 0)
+            ed(i - 2, 3)
+            ab(i - 2, 2)
+            root(i)
             cp(i + 2, 1)
-            for a in range(4):
-                mx(i + 1, a)
+            mx(i + 1, 2)
+            mx(i + 1, 3)
             tau(i)
+            ab(i - 2, 3)
             ed(i - 1, 0)
-            ab(i - 1, 0)
+            t1(i + 3, 1)
             qz(i + 2)
             rec(i)
             ed(i - 1, 1)
-        ab(NG - 2, 1)
-        ed(NG - 2, 2)
-        wg(NG - 1, 0)
-        wv(NG - 1, 1)
-        wv(NG - 1, 2)
-        wv(NG - 1, 3)
-        ed(NG - 2, 3)
-        ab(NG - 2, 2)
-        pull(NG - 2, 3)
+        i = NG - 1
+        ab(i - 2, 0)
+        p1(i, 0)
+        p2(i, 0)
+        wg(i - 1, 0)
+        p1(i, 1)
+        p2(i, 1)
+        stir(i)
+        wg(i - 1, 1)
+        ed(i - 2, 2)
+        ab(i - 2, 1)
+        p1(i, 2)
+        p2(i, 2)
+        stir(i)
+        wg(i - 1, 2)
+        ed(i - 2, 3)
+        p1(i, 3)
+        sg(i)
+        p2(i, 3)
+        root(i)
+        stir(i)
+        stir(i)
+        wg(i - 1, 3)
+        tau(i)
+        rec(i)
+        ab(i - 2, 2)
+        ab(i - 2, 3)
         for j in range(4):
-            ed(NG - 1, j)
+            ed(i - 1, j)
+        wv(i, 3)
+        wv(i, 0)
+        wv(i, 1)
+        wv(i, 2)
         seam_edges()
-        ab(NG - 1, 0)
-        pull(NG - 1, 1)
-        av(NG - 2, 3)
-        ab(NG - 1, 2)
-        pull(NG - 1, 3)
-        av(NG - 1, 1)
+        for j in range(4):
+            ed(i, j)
+        ab(i - 1, 0)
+        ab(i - 1, 1)
+        ab(i - 1, 2)
+        pull(i - 1, 3)
         seam_pull()
-        av(NG - 1, 3)
+        av(i - 1, 3)
         seam_sum()
+        for j in range(4):
+            ab(i, j)
 
         dcol = small.tile([P, 4], F32, tag="dcol", name="dcol")
         nc.vector.tensor_reduce(out=dcol[:], in_=part[:].rearrange("p g j -> p j g"), axis=AX.X, op=ALU.add)

@@ -63,7 +63,8 @@ def tile_dispatcher_pa_kernel(tc, inv, Wk, bk, out):
                 out=turn[:, a : a + 1], in0=one[:], scalar1=(1.0 if a % 2 == 0 else -1.0) / EPS, scalar2=None, op0=ALU.mult
             )
         bias = const.tile([P, D], F32, name="bias")
-        part = const.tile([P, NG + 1, 4], F32, name="part")
+        part = const.tile([P, 4, NG], F32, name="part")
+        seam_part = const.tile([P, 4], F32, name="seam_part")
         w_first = const.tile([P, D], F32, name="w_first")
         w_codes = const.tile([P, D], U32, name="w_codes", align_bytes=64)
         w_scl = const.tile([P, D], U8, name="w_scl", align_bytes=64)
@@ -106,15 +107,16 @@ def tile_dispatcher_pa_kernel(tc, inv, Wk, bk, out):
         def mx(g, a):
             if ok(g):
                 acc = psum.tile([P, D], F32, tag="acc", name="acc", bufs=4)
-                nc.tensor.matmul_mx(
-                    out=acc[:],
-                    lhsT=st[("codes", g)][:, a * P : (a + 1) * P].bitcast(FP8X4),
-                    lhsT_scale=st[("scl", g)][:, a * P : (a + 1) * P],
-                    rhs=w_codes[:].bitcast(FP8X4),
-                    rhs_scale=w_scl[:],
-                    start=True,
-                    stop=True,
-                )
+                for n in range(2 if a % 2 == 0 else 1):
+                    nc.tensor.matmul_mx(
+                        out=acc[:],
+                        lhsT=st[("codes", g)][:, a * P : (a + 1) * P].bitcast(FP8X4),
+                        lhsT_scale=st[("scl", g)][:, a * P : (a + 1) * P],
+                        rhs=w_codes[:].bitcast(FP8X4),
+                        rhs_scale=w_scl[:],
+                        start=True,
+                        stop=True,
+                    )
                 st[("acc", g, a)] = acc
 
         def stir(g):
@@ -172,7 +174,7 @@ def tile_dispatcher_pa_kernel(tc, inv, Wk, bk, out):
         def sg(g):
             if ok(g):
                 sx = small.tile([P, 4], F32, tag="sx", name="sx")
-                nc.gpsimd.tensor_tensor(out=sx[:], in0=st[("ssum", g)][:], in1=turn[:], op=ALU.mult)
+                nc.vector.tensor_tensor(out=sx[:], in0=st[("ssum", g)][:], in1=turn[:], op=ALU.mult)
                 st[("sx", g)] = sx
 
         def rec(g):
@@ -222,13 +224,13 @@ def tile_dispatcher_pa_kernel(tc, inv, Wk, bk, out):
             if ok(g):
                 if g == NG - 1:
                     eb = psum.tile([P, 4, P], F32, tag="acc", name="eb", bufs=4)
-                elif g == NG - 2 and j >= 2:
+                elif g == NG - 2 and j < 2:
                     eb = psum.tile([P, 4, P], F32, tag="xt", name="eb")
                 else:
                     eb = psum.tile([P, 4, P], F32, tag="e", name="eb")
                 for q in range(4):
                     if 4 * g + q >= 1:
-                        add_flipped(eb[:, q, :], st[("w", 4 * g + q - 1)], st[("w", 4 * g + q)], ident, j, q == 1 and j in (1, 3))
+                        add_flipped(eb[:, q, :], st[("w", 4 * g + q - 1)], st[("w", 4 * g + q)], ident, j, q == 1 and j == 1)
                 st[("e", g, j)] = eb
 
         def ab(g, j):
@@ -237,7 +239,7 @@ def tile_dispatcher_pa_kernel(tc, inv, Wk, bk, out):
                 lo = P if g == 0 else 0
                 junk = work.tile([P, D], F32, tag="junk", name="junk")
                 nc.scalar.activation(
-                    out=junk[:, lo:D], in_=flat[:, lo:D], func=ACT.Abs, accum_out=part[:, g, j : j + 1]
+                    out=junk[:, lo:D], in_=flat[:, lo:D], func=ACT.Abs, accum_out=part[:, j, g : g + 1]
                 )
 
         def pull(g, j):
@@ -249,7 +251,7 @@ def tile_dispatcher_pa_kernel(tc, inv, Wk, bk, out):
         def av(g, j):
             if ok(g):
                 nc.vector.tensor_reduce(
-                    out=part[:, g, j : j + 1],
+                    out=part[:, j, g : g + 1],
                     in_=st[("keep", g, j)][:],
                     axis=AX.X,
                     op=ALU.add,
@@ -270,7 +272,7 @@ def tile_dispatcher_pa_kernel(tc, inv, Wk, bk, out):
 
         def seam_sum():
             nc.vector.tensor_reduce(
-                out=part[:, NG, :], in_=st["keep"][:], axis=AX.X, op=ALU.add, apply_absolute_value=True
+                out=seam_part[:], in_=st["keep"][:], axis=AX.X, op=ALU.add, apply_absolute_value=True
             )
 
         hot = psum.tile([P, 2, 2, P], F32, tag="xt", name="hot")
@@ -287,13 +289,28 @@ def tile_dispatcher_pa_kernel(tc, inv, Wk, bk, out):
         nc.vector.quantize_mx(out=w_codes[:].bitcast(FP8X4), scales=w_scl[:], in_=grp_w[:])
         nc.vector.tensor_copy(out=bias[:], in_=b_bf[:])
 
-        for i in range(-3, NG - 1):
+        for g in range(2):
+            for h in range(2):
+                t1(g, h)
+                cp(g, h)
+            if g == 0:
+                qz(0)
+        for a in range(4):
+            mx(0, a)
+        for h in range(2):
+            t1(2, h)
+        for i in range(NG - 1):
             ab(i - 2, 0)
             p1(i, 0)
+            if i == 0:
+                qz(1)
             p2(i, 0)
             wg(i - 1, 0)
             p1(i, 1)
             p2(i, 1)
+            if i == 0:
+                cp(2, 0)
+                t1(3, 0)
             mx(i + 1, 0)
             mx(i + 1, 1)
             wg(i - 1, 1)
@@ -304,11 +321,11 @@ def tile_dispatcher_pa_kernel(tc, inv, Wk, bk, out):
             wg(i - 1, 2)
             p1(i, 3)
             p2(i, 3)
-            sg(i)
             wg(i - 1, 3)
-            cp(i + 2, 0)
-            t1(i + 3, 0)
-            ed(i - 2, 3)
+            if i > 0:
+                cp(i + 2, 0)
+                ed(i - 2, 3)
+                t1(i + 3, 0)
             ab(i - 2, 2)
             root(i)
             cp(i + 2, 1)
@@ -318,6 +335,7 @@ def tile_dispatcher_pa_kernel(tc, inv, Wk, bk, out):
             ab(i - 2, 3)
             ed(i - 1, 0)
             t1(i + 3, 1)
+            sg(i)
             qz(i + 2)
             rec(i)
             ed(i - 1, 1)
@@ -338,13 +356,12 @@ def tile_dispatcher_pa_kernel(tc, inv, Wk, bk, out):
         wg(i - 1, 2)
         ed(i - 2, 3)
         p1(i, 3)
-        sg(i)
         p2(i, 3)
         root(i)
         stir(i)
-        stir(i)
         wg(i - 1, 3)
         tau(i)
+        sg(i)
         rec(i)
         ab(i - 2, 2)
         ab(i - 2, 3)
@@ -359,21 +376,42 @@ def tile_dispatcher_pa_kernel(tc, inv, Wk, bk, out):
             ed(i, j)
         ab(i - 1, 0)
         ab(i - 1, 1)
-        ab(i - 1, 2)
+        pull(i - 1, 2)
         pull(i - 1, 3)
+        av(i - 1, 2)
         seam_pull()
         av(i - 1, 3)
         seam_sum()
         for j in range(4):
             ab(i, j)
 
-        dcol = small.tile([P, 4], F32, tag="dcol", name="dcol")
-        nc.vector.tensor_reduce(out=dcol[:], in_=part[:].rearrange("p g j -> p j g"), axis=AX.X, op=ALU.add)
-        fin = psum.tile([P, D], F32, tag="xt", name="fin")
-        for j in range(4):
-            nc.tensor.transpose(fin[:, j * P : (j + 1) * P], dcol[:, j : j + 1].to_broadcast([P, P]), ident[:])
         res = const.tile([P, D], F32, name="res")
-        nc.vector.tensor_copy(out=res[:], in_=fin[:])
-        for a in range(4):
-            eng = nc.sync if a % 2 == 0 else nc.scalar
-            eng.dma_start(out=out[a * P : (a + 1) * P, :], in_=res[:])
+
+        def total(lo, hi):
+            n = hi - lo
+            some = small.tile([P, n], F32, tag="some%d" % n, name="some")
+            nc.vector.tensor_reduce(out=some[:], in_=part[:, lo:hi, :], axis=AX.X, op=ALU.add)
+            dcol = small.tile([P, n], F32, tag="dcol%d" % n, name="dcol")
+            nc.vector.tensor_tensor(out=dcol[:], in0=some[:], in1=seam_part[:, lo:hi], op=ALU.add)
+            for j in range(lo, hi):
+                st[("d", j)] = dcol[:, j - lo : j - lo + 1]
+
+        def turn_up(j):
+            if j in (0, 3):
+                st["fin"] = psum.tile([P, 3, P], F32, tag="xt", name="fin")
+            nc.tensor.transpose(st["fin"][:, j % 3, :], st[("d", j)].to_broadcast([P, P]), ident[:])
+
+        def show(lo, hi):
+            cols = slice(lo * P, hi * P)
+            nc.vector.tensor_copy(out=res[:, cols], in_=st["fin"][:, 0 : hi - lo, :].rearrange("p j r -> p (j r)"))
+            for a in range(4):
+                eng = nc.sync if a % 2 == 0 else nc.scalar
+                eng.dma_start(out=out[a * P : (a + 1) * P, cols], in_=res[:, cols])
+
+        total(0, 3)
+        total(3, 4)
+        for j in range(3):
+            turn_up(j)
+        show(0, 3)
+        turn_up(3)
+        show(3, 4)

@@ -57,11 +57,6 @@ def tile_dispatcher_pa_kernel(tc, inv, Wk, bk, out):
         shift = const.tile([P, P], F32, name="shift")
         nc.vector.tensor_copy(out=shift[:, 1:P], in_=ident[:, 0 : P - 1])
         nc.vector.tensor_copy(out=shift[:, 0:1], in_=ident[:, P - 1 : P])
-        turn = const.tile([P, 4], F32, name="turn")
-        for a in range(4):
-            nc.vector.tensor_scalar(
-                out=turn[:, a : a + 1], in0=one[:], scalar1=(1.0 if a % 2 == 0 else -1.0) / EPS, scalar2=None, op0=ALU.mult
-            )
         bias = const.tile([P, D], F32, name="bias")
         part = const.tile([P, 4, NG], F32, name="part")
         seam_part = const.tile([P, 4], F32, name="seam_part")
@@ -90,7 +85,7 @@ def tile_dispatcher_pa_kernel(tc, inv, Wk, bk, out):
                 if h == 0:
                     st[("grp", g)] = work.tile([P, 4 * D], BF16, tag="grp", name="grp", align_bytes=64)
                 grp = st[("grp", g)][:, 2 * h * D : (2 * h + 2) * D]
-                move = nc.scalar.copy if g < 3 else nc.vector.tensor_copy
+                move = nc.scalar.copy if g < 3 or h == 0 or g % 2 == 0 else nc.vector.tensor_copy
                 move(
                     out=grp.bitcast(F32).rearrange("p (a r u) -> p a r u", a=2, r=P, u=2),
                     in_=st[("xt", g, h)][:].rearrange("p h u r -> p h r u"),
@@ -107,7 +102,7 @@ def tile_dispatcher_pa_kernel(tc, inv, Wk, bk, out):
         def mx(g, a):
             if ok(g):
                 acc = psum.tile([P, D], F32, tag="acc", name="acc", bufs=4)
-                for n in range(2 if a % 2 == 0 else 1):
+                for n in range(1):
                     nc.tensor.matmul_mx(
                         out=acc[:],
                         lhsT=st[("codes", g)][:, a * P : (a + 1) * P].bitcast(FP8X4),
@@ -171,17 +166,11 @@ def tile_dispatcher_pa_kernel(tc, inv, Wk, bk, out):
                 nc.scalar.activation(out=rn[:], in_=st[("n2", g)][:], func=ACT.Abs_reciprocal_sqrt, bias=1e-30)
                 st[("rn", g)] = rn
 
-        def sg(g):
-            if ok(g):
-                sx = small.tile([P, 4], F32, tag="sx", name="sx")
-                nc.vector.tensor_tensor(out=sx[:], in0=st[("ssum", g)][:], in1=turn[:], op=ALU.mult)
-                st[("sx", g)] = sx
-
         def rec(g):
             if ok(g):
                 r2 = small.tile([P, 4], F32, tag="r2", name="r2")
                 nc.vector.scalar_tensor_tensor(
-                    out=r2[:], in0=st[("rn", g)][:], scalar=1.0 / EPS, in1=st[("sx", g)][:], op0=ALU.min, op1=ALU.mult
+                    out=r2[:], in0=st[("rn", g)][:], scalar=1.0 / EPS, in1=st[("ssum", g)][:], op0=ALU.min, op1=ALU.mult
                 )
                 st[("r2", g)] = r2
 
@@ -195,14 +184,11 @@ def tile_dispatcher_pa_kernel(tc, inv, Wk, bk, out):
                     out=ww[:],
                     in0=st[("tau", g)][:, a, :],
                     scalar1=st[("r2", g)][:, a : a + 1],
-                    scalar2=0.0,
+                    scalar2=(1.0 / EPS if a % 2 == 0 else -1.0 / EPS),
                     op0=ALU.mult,
-                    op1=ALU.add,
+                    op1=ALU.mult,
                 )
                 st[("w", 4 * g + a)] = ww
-
-        def wg(g, a):
-            wt(g, a, nc.gpsimd)
 
         def wv(g, a):
             wt(g, a, nc.vector)
@@ -230,7 +216,7 @@ def tile_dispatcher_pa_kernel(tc, inv, Wk, bk, out):
                     eb = psum.tile([P, 4, P], F32, tag="e", name="eb")
                 for q in range(4):
                     if 4 * g + q >= 1:
-                        add_flipped(eb[:, q, :], st[("w", 4 * g + q - 1)], st[("w", 4 * g + q)], ident, j, q == 1 and j == 1)
+                        add_flipped(eb[:, q, :], st[("w", 4 * g + q - 1)], st[("w", 4 * g + q)], ident, j, q == 1)
                 st[("e", g, j)] = eb
 
         def ab(g, j):
@@ -300,72 +286,64 @@ def tile_dispatcher_pa_kernel(tc, inv, Wk, bk, out):
         for h in range(2):
             t1(2, h)
         for i in range(NG - 1):
-            ab(i - 2, 0)
             p1(i, 0)
             if i == 0:
                 qz(1)
             p2(i, 0)
-            wg(i - 1, 0)
+            ab(i - 2, 2)
+            wv(i - 1, 0)
+            wv(i - 1, 1)
+            ed(i - 2, 3)
             p1(i, 1)
             p2(i, 1)
-            if i == 0:
-                cp(2, 0)
-                t1(3, 0)
-            mx(i + 1, 0)
-            mx(i + 1, 1)
-            wg(i - 1, 1)
-            ab(i - 2, 1)
+            if i > 0:
+                t1(i + 2, 0)
+                t1(i + 2, 1)
+            ab(i - 2, 3)
+            wv(i - 1, 2)
+            wv(i - 1, 3)
             p1(i, 2)
             p2(i, 2)
-            ed(i - 2, 2)
-            wg(i - 1, 2)
-            p1(i, 3)
-            p2(i, 3)
-            wg(i - 1, 3)
-            if i > 0:
-                cp(i + 2, 0)
-                ed(i - 2, 3)
-                t1(i + 3, 0)
-            ab(i - 2, 2)
-            root(i)
-            cp(i + 2, 1)
-            mx(i + 1, 2)
-            mx(i + 1, 3)
-            tau(i)
-            ab(i - 2, 3)
             ed(i - 1, 0)
-            t1(i + 3, 1)
-            sg(i)
-            qz(i + 2)
-            rec(i)
+            ab(i - 1, 0)
             ed(i - 1, 1)
+            p1(i, 3)
+            if i > 0:
+                qz(i + 1)
+            p2(i, 3)
+            root(i)
+            for a in range(4):
+                mx(i + 1, a)
+            ab(i - 1, 1)
+            cp(i + 2, 0)
+            tau(i)
+            cp(i + 2, 1)
+            rec(i)
+            ed(i - 1, 2)
         i = NG - 1
-        ab(i - 2, 0)
         p1(i, 0)
         p2(i, 0)
-        wg(i - 1, 0)
+        wv(i - 1, 0)
+        wv(i - 1, 1)
+        ed(i - 2, 3)
         p1(i, 1)
         p2(i, 1)
+        ab(i - 2, 2)
+        wv(i - 1, 2)
+        wv(i - 1, 3)
         stir(i)
-        wg(i - 1, 1)
-        ed(i - 2, 2)
-        ab(i - 2, 1)
         p1(i, 2)
         p2(i, 2)
         stir(i)
-        wg(i - 1, 2)
-        ed(i - 2, 3)
+        for j in range(2):
+            ed(i - 1, j)
         p1(i, 3)
         p2(i, 3)
         root(i)
-        stir(i)
-        wg(i - 1, 3)
         tau(i)
-        sg(i)
         rec(i)
-        ab(i - 2, 2)
         ab(i - 2, 3)
-        for j in range(4):
+        for j in range(2, 4):
             ed(i - 1, j)
         wv(i, 3)
         wv(i, 0)

@@ -85,7 +85,7 @@ def tile_dispatcher_pa_kernel(tc, inv, Wk, bk, out):
                 if h == 0:
                     st[("grp", g)] = work.tile([P, 4 * D], BF16, tag="grp", name="grp", align_bytes=64)
                 grp = st[("grp", g)][:, 2 * h * D : (2 * h + 2) * D]
-                move = nc.scalar.copy if g < 3 or h == 0 or g % 2 == 0 else nc.vector.tensor_copy
+                move = nc.scalar.copy if True else nc.vector.tensor_copy
                 move(
                     out=grp.bitcast(F32).rearrange("p (a r u) -> p a r u", a=2, r=P, u=2),
                     in_=st[("xt", g, h)][:].rearrange("p h u r -> p h r u"),
@@ -144,7 +144,7 @@ def tile_dispatcher_pa_kernel(tc, inv, Wk, bk, out):
 
         def p2(g, a):
             if ok(g):
-                junk = work.tile([P, D], F32, tag="junk", name="junk")
+                junk = work.tile([P, D], F32, tag="junk", name="junk", bufs=12)
                 nc.scalar.activation(
                     out=junk[:],
                     in_=st[("o", g)][:, a, :],
@@ -223,7 +223,7 @@ def tile_dispatcher_pa_kernel(tc, inv, Wk, bk, out):
             if ok(g):
                 flat = st[("e", g, j)][:].rearrange("p q r -> p (q r)")
                 lo = P if g == 0 else 0
-                junk = work.tile([P, D], F32, tag="junk", name="junk")
+                junk = work.tile([P, D], F32, tag="junk", name="junk", bufs=12)
                 nc.scalar.activation(
                     out=junk[:, lo:D], in_=flat[:, lo:D], func=ACT.Abs, accum_out=part[:, j, g : g + 1]
                 )
@@ -291,43 +291,44 @@ def tile_dispatcher_pa_kernel(tc, inv, Wk, bk, out):
                 qz(1)
             p2(i, 0)
             ab(i - 2, 2)
-            wv(i - 1, 0)
-            wv(i - 1, 1)
+            rec(i - 1)
             ed(i - 2, 3)
             p1(i, 1)
             p2(i, 1)
+            wv(i - 1, 0)
+            wv(i - 1, 1)
             if i > 0:
                 t1(i + 2, 0)
                 t1(i + 2, 1)
             ab(i - 2, 3)
-            wv(i - 1, 2)
-            wv(i - 1, 3)
             p1(i, 2)
             p2(i, 2)
+            wv(i - 1, 2)
+            wv(i - 1, 3)
+            cp(i + 2, 0)
             ed(i - 1, 0)
-            ab(i - 1, 0)
-            ed(i - 1, 1)
             p1(i, 3)
+            p2(i, 3)
             if i > 0:
                 qz(i + 1)
-            p2(i, 3)
+            ed(i - 1, 1)
+            ab(i - 1, 0)
             root(i)
             for a in range(4):
                 mx(i + 1, a)
-            ab(i - 1, 1)
-            cp(i + 2, 0)
             tau(i)
             cp(i + 2, 1)
-            rec(i)
+            ab(i - 1, 1)
             ed(i - 1, 2)
         i = NG - 1
         p1(i, 0)
         p2(i, 0)
-        wv(i - 1, 0)
-        wv(i - 1, 1)
+        rec(i - 1)
         ed(i - 2, 3)
         p1(i, 1)
         p2(i, 1)
+        wv(i - 1, 0)
+        wv(i - 1, 1)
         ab(i - 2, 2)
         wv(i - 1, 2)
         wv(i - 1, 3)

@@ -33,12 +33,15 @@ def tile_dispatcher_pa_kernel(tc, inv, Wk, bk, out):
         psum = ctx.enter_context(tc.psum_pool(name="psum", bufs=2))
         ctx.enter_context(tc.manual_schedule())
 
-        b_bf = const.tile([P, D], BF16, name="b_bf")
-        nc.scalar.dma_start(out=b_bf[:], in_=bk.partition_broadcast(P))
+        b_row = const.tile([P, D], BF16, name="b_row")
+        nc.vector.memset(b_row[:].bitcast(F32), 0.0)
+        ones = const.tile([P, P], BF16, name="ones")
+        nc.vector.memset(ones[:], 1.0)
         w_sb = const.tile([P, 4, D], BF16, name="w_sb")
         w_rows = Wk.rearrange("(a p) k -> p a k", p=P)
         for h in range(2):
             nc.sync.dma_start(out=w_sb[:, 2 * h : 2 * h + 2, :], in_=w_rows[:, 2 * h : 2 * h + 2, :])
+        nc.sync.dma_start(out=b_row[0:1, :], in_=bk.unsqueeze(0))
         xs = []
         for g in range(NG):
             xg = const.tile([P, 4, D], BF16, name="x%d" % g)
@@ -85,17 +88,23 @@ def tile_dispatcher_pa_kernel(tc, inv, Wk, bk, out):
                 if h == 0:
                     st[("grp", g)] = work.tile([P, 4 * D], BF16, tag="grp", name="grp", align_bytes=64)
                 grp = st[("grp", g)][:, 2 * h * D : (2 * h + 2) * D]
-                move = nc.scalar.copy if True else nc.vector.tensor_copy
+                move = nc.scalar.copy if g < 3 or h == 0 or g % 2 == 0 else nc.vector.tensor_copy
                 move(
                     out=grp.bitcast(F32).rearrange("p (a r u) -> p a r u", a=2, r=P, u=2),
                     in_=st[("xt", g, h)][:].rearrange("p h u r -> p h r u"),
                 )
 
-        def qz(g):
+        def qz(g, parts=1):
             if ok(g):
                 codes = work.tile([P, 4 * P], U32, tag="codes", name="codes", align_bytes=64)
                 scl = work.tile([P, 4 * P], U8, tag="scl", name="scl", align_bytes=64)
-                nc.vector.quantize_mx(out=codes[:].bitcast(FP8X4), scales=scl[:], in_=st[("grp", g)][:])
+                n = 4 * P // parts
+                for c in range(0, 4 * P, n):
+                    nc.vector.quantize_mx(
+                        out=codes[:, c : c + n].bitcast(FP8X4),
+                        scales=scl[:, c : c + n],
+                        in_=st[("grp", g)][:, 4 * c : 4 * (c + n)],
+                    )
                 st[("codes", g)] = codes
                 st[("scl", g)] = scl
 
@@ -216,7 +225,7 @@ def tile_dispatcher_pa_kernel(tc, inv, Wk, bk, out):
                     eb = psum.tile([P, 4, P], F32, tag="e", name="eb")
                 for q in range(4):
                     if 4 * g + q >= 1:
-                        add_flipped(eb[:, q, :], st[("w", 4 * g + q - 1)], st[("w", 4 * g + q)], ident, j, q == 1)
+                        add_flipped(eb[:, q, :], st[("w", 4 * g + q - 1)], st[("w", 4 * g + q)], ident, j, q == 1 and j != 1 and (g < NG - 1 or j == 0))
                 st[("e", g, j)] = eb
 
         def ab(g, j):
@@ -262,7 +271,7 @@ def tile_dispatcher_pa_kernel(tc, inv, Wk, bk, out):
             )
 
         hot = psum.tile([P, 2, 2, P], F32, tag="xt", name="hot")
-        for n in range(6):
+        for n in range(3):
             nc.tensor.matmul(out=hot[:, 0, 0, :], lhsT=ident[:], rhs=ident[:], start=True, stop=True)
         grp_w = const.tile([P, 4 * D], BF16, name="grp_w", align_bytes=64)
         for h in range(2):
@@ -273,23 +282,27 @@ def tile_dispatcher_pa_kernel(tc, inv, Wk, bk, out):
                 in_=wb[:].rearrange("p h u r -> p h r u"),
             )
         nc.vector.quantize_mx(out=w_codes[:].bitcast(FP8X4), scales=w_scl[:], in_=grp_w[:])
-        nc.vector.tensor_copy(out=bias[:], in_=b_bf[:])
+        b_bank = psum.tile([P, D], F32, tag="acc", name="b_bank", bufs=4)
+        nc.tensor.matmul(out=b_bank[:], lhsT=ones[:], rhs=b_row[:], start=True, stop=True)
 
-        for g in range(2):
-            for h in range(2):
-                t1(g, h)
-                cp(g, h)
-            if g == 0:
-                qz(0)
-        for a in range(4):
-            mx(0, a)
         for h in range(2):
-            t1(2, h)
+            t1(0, h)
+            cp(0, h)
+        qz(0, 2)
+        nc.vector.tensor_copy(out=bias[:], in_=b_bank[:])
+        t1(1, 0)
+        cp(1, 0)
+        mx(0, 0)
+        mx(0, 1)
+        t1(1, 1)
+        mx(0, 2)
+        mx(0, 3)
+        t1(2, 0)
         for i in range(NG - 1):
             p1(i, 0)
-            if i == 0:
-                qz(1)
             p2(i, 0)
+            if i == 0:
+                cp(1, 1)
             ab(i - 2, 2)
             rec(i - 1)
             ed(i - 2, 3)
@@ -297,11 +310,15 @@ def tile_dispatcher_pa_kernel(tc, inv, Wk, bk, out):
             p2(i, 1)
             wv(i - 1, 0)
             wv(i - 1, 1)
-            if i > 0:
+            if i == 0:
+                t1(2, 1)
+            else:
                 t1(i + 2, 0)
                 t1(i + 2, 1)
             ab(i - 2, 3)
             p1(i, 2)
+            if i == 0:
+                qz(1)
             p2(i, 2)
             wv(i - 1, 2)
             wv(i - 1, 3)
@@ -353,11 +370,9 @@ def tile_dispatcher_pa_kernel(tc, inv, Wk, bk, out):
         seam_edges()
         for j in range(4):
             ed(i, j)
-        ab(i - 1, 0)
-        ab(i - 1, 1)
-        pull(i - 1, 2)
+        for j in range(3):
+            ab(i - 1, j)
         pull(i - 1, 3)
-        av(i - 1, 2)
         seam_pull()
         av(i - 1, 3)
         seam_sum()
@@ -366,31 +381,29 @@ def tile_dispatcher_pa_kernel(tc, inv, Wk, bk, out):
 
         res = const.tile([P, D], F32, name="res")
 
-        def total(lo, hi):
-            n = hi - lo
-            some = small.tile([P, n], F32, tag="some%d" % n, name="some")
-            nc.vector.tensor_reduce(out=some[:], in_=part[:, lo:hi, :], axis=AX.X, op=ALU.add)
-            dcol = small.tile([P, n], F32, tag="dcol%d" % n, name="dcol")
-            nc.vector.tensor_tensor(out=dcol[:], in0=some[:], in1=seam_part[:, lo:hi], op=ALU.add)
-            for j in range(lo, hi):
-                st[("d", j)] = dcol[:, j - lo : j - lo + 1]
-
-        def turn_up(j):
-            if j in (0, 3):
-                st["fin"] = psum.tile([P, 3, P], F32, tag="xt", name="fin")
-            nc.tensor.transpose(st["fin"][:, j % 3, :], st[("d", j)].to_broadcast([P, P]), ident[:])
-
-        def show(lo, hi):
-            cols = slice(lo * P, hi * P)
-            nc.vector.tensor_copy(out=res[:, cols], in_=st["fin"][:, 0 : hi - lo, :].rearrange("p j r -> p (j r)"))
+        for lo in (0, 2):
+            cols = slice(lo * P, (lo + 2) * P)
+            dcol = small.tile([P, 2], F32, tag="dcol", name="dcol")
+            nc.vector.tensor_reduce(out=dcol[:], in_=part[:, lo : lo + 2, :], axis=AX.X, op=ALU.add)
+            fin = psum.tile([P, 2, P], F32, tag="xt", name="fin")
+            for j in range(2):
+                nc.tensor.matmul(
+                    out=fin[:, j, :],
+                    lhsT=seam_part[:, lo + j : lo + j + 1].to_broadcast([P, P]),
+                    rhs=ident[:],
+                    is_transpose=True,
+                    start=True,
+                    stop=False,
+                )
+                nc.tensor.matmul(
+                    out=fin[:, j, :],
+                    lhsT=dcol[:, j : j + 1].to_broadcast([P, P]),
+                    rhs=ident[:],
+                    is_transpose=True,
+                    start=False,
+                    stop=True,
+                )
+            nc.vector.tensor_copy(out=res[:, cols], in_=fin[:].rearrange("p j r -> p (j r)"))
             for a in range(4):
                 eng = nc.sync if a % 2 == 0 else nc.scalar
                 eng.dma_start(out=out[a * P : (a + 1) * P, cols], in_=res[:, cols])
-
-        total(0, 3)
-        total(3, 4)
-        for j in range(3):
-            turn_up(j)
-        show(0, 3)
-        turn_up(3)
-        show(3, 4)

@@ -88,7 +88,7 @@ def tile_dispatcher_pa_kernel(tc, inv, Wk, bk, out):
                 if h == 0:
                     st[("grp", g)] = work.tile([P, 4 * D], BF16, tag="grp", name="grp", align_bytes=64)
                 grp = st[("grp", g)][:, 2 * h * D : (2 * h + 2) * D]
-                move = nc.scalar.copy if g < 3 or h == 0 or g % 2 == 0 else nc.vector.tensor_copy
+                move = nc.scalar.copy if g < 3 or h == 0 else nc.vector.tensor_copy
                 move(
                     out=grp.bitcast(F32).rearrange("p (a r u) -> p a r u", a=2, r=P, u=2),
                     in_=st[("xt", g, h)][:].rearrange("p h u r -> p h r u"),
@@ -193,14 +193,14 @@ def tile_dispatcher_pa_kernel(tc, inv, Wk, bk, out):
                     out=ww[:],
                     in0=st[("tau", g)][:, a, :],
                     scalar1=st[("r2", g)][:, a : a + 1],
-                    scalar2=(1.0 / EPS if a % 2 == 0 else -1.0 / EPS),
+                    scalar2=(0.0 if eng is nc.gpsimd else 1.0 if a % 2 == 0 else -1.0),
                     op0=ALU.mult,
-                    op1=ALU.mult,
+                    op1=(ALU.add if eng is nc.gpsimd else ALU.mult),
                 )
                 st[("w", 4 * g + a)] = ww
 
         def wv(g, a):
-            wt(g, a, nc.vector)
+            wt(g, a, nc.gpsimd if a % 2 == 0 and g < NG - 1 else nc.vector)
 
         def add_flipped(dst, first, second, perm, j, plain):
             nc.tensor.matmul(
@@ -225,7 +225,7 @@ def tile_dispatcher_pa_kernel(tc, inv, Wk, bk, out):
                     eb = psum.tile([P, 4, P], F32, tag="e", name="eb")
                 for q in range(4):
                     if 4 * g + q >= 1:
-                        add_flipped(eb[:, q, :], st[("w", 4 * g + q - 1)], st[("w", 4 * g + q)], ident, j, q == 1 and j != 1 and (g < NG - 1 or j == 0))
+                        add_flipped(eb[:, q, :], st[("w", 4 * g + q - 1)], st[("w", 4 * g + q)], ident, j, q == 1 and j in (0, 3) and (g < NG - 1 or j == 0))
                 st[("e", g, j)] = eb
 
         def ab(g, j):
@@ -305,27 +305,25 @@ def tile_dispatcher_pa_kernel(tc, inv, Wk, bk, out):
                 cp(1, 1)
             ab(i - 2, 2)
             rec(i - 1)
+            wv(i - 1, 0)
+            wv(i - 1, 2)
+            if i > 0:
+                t1(i + 2, 0)
             ed(i - 2, 3)
             p1(i, 1)
             p2(i, 1)
-            wv(i - 1, 0)
-            wv(i - 1, 1)
-            if i == 0:
-                t1(2, 1)
-            else:
-                t1(i + 2, 0)
-                t1(i + 2, 1)
+            t1(i + 2, 1)
             ab(i - 2, 3)
             p1(i, 2)
             if i == 0:
                 qz(1)
             p2(i, 2)
-            wv(i - 1, 2)
+            p1(i, 3)
+            p2(i, 3)
+            wv(i - 1, 1)
             wv(i - 1, 3)
             cp(i + 2, 0)
             ed(i - 1, 0)
-            p1(i, 3)
-            p2(i, 3)
             if i > 0:
                 qz(i + 1)
             ed(i - 1, 1)
@@ -403,7 +401,13 @@ def tile_dispatcher_pa_kernel(tc, inv, Wk, bk, out):
                     start=False,
                     stop=True,
                 )
-            nc.vector.tensor_copy(out=res[:, cols], in_=fin[:].rearrange("p j r -> p (j r)"))
+            nc.vector.tensor_scalar(
+                out=res[:, cols],
+                in0=fin[:].rearrange("p j r -> p (j r)"),
+                scalar1=1.0 / EPS,
+                scalar2=None,
+                op0=ALU.mult,
+            )
             for a in range(4):
                 eng = nc.sync if a % 2 == 0 else nc.scalar
                 eng.dma_start(out=out[a * P : (a + 1) * P, cols], in_=res[:, cols])

import math
from contextlib import ExitStack

import concourse.mybir as mybir
from concourse.masks import make_identity

FLOPS = 2 * 8192 * 512 * 512

F32 = mybir.dt.float32
BF16 = mybir.dt.bfloat16
U32 = mybir.dt.uint32
U8 = mybir.dt.uint8
FP8X4 = mybir.dt.float8_e4m3fn_x4
ALU = mybir.AluOpType
ACT = mybir.ActivationFunctionType
AX = mybir.AxisListType

P = 128
D = 512
NT = 64
NG = 16
EPS = 1e-8
DELTA = EPS / math.sqrt(D)


def tile_dispatcher_pa_kernel(tc, inv, Wk, bk, out):
    nc = tc.nc
    rows = inv.flatten_outer_dims().rearrange("(p t) k -> p t k", t=NT)
    with ExitStack() as ctx:
        const = ctx.enter_context(tc.tile_pool(name="const", bufs=1))
        work = ctx.enter_context(tc.tile_pool(name="work", bufs=3))
        small = ctx.enter_context(tc.tile_pool(name="small", bufs=3))
        psum = ctx.enter_context(tc.psum_pool(name="psum", bufs=2))
        ctx.enter_context(tc.manual_schedule())

        b_row = const.tile([P, D], BF16, name="b_row")
        nc.vector.memset(b_row[:].bitcast(F32), 0.0)
        ones = const.tile([P, P], BF16, name="ones")
        nc.vector.memset(ones[:], 1.0)
        w_sb = const.tile([P, 4, D], BF16, name="w_sb")
        w_rows = Wk.rearrange("(a p) k -> p a k", p=P)
        for h in range(2):
            nc.sync.dma_start(out=w_sb[:, 2 * h : 2 * h + 2, :], in_=w_rows[:, 2 * h : 2 * h + 2, :])
        nc.sync.dma_start(out=b_row[0:1, :], in_=bk.unsqueeze(0))
        xs = []
        for g in range(NG):
            xg = const.tile([P, 4, D], BF16, name="x%d" % g)
            if g == 0:
                for h in range(2):
                    nc.sync.dma_start(out=xg[:, 2 * h : 2 * h + 2, :], in_=rows[:, 2 * h : 2 * h + 2, :])
            else:
                nc.sync.dma_start(out=xg[:], in_=rows[:, 4 * g : 4 * g + 4, :])
            xs.append(xg)
        one = const.tile([P, 1], F32, name="one")
        nc.vector.memset(one[:], 1.0)
        warm = const.tile([P, 1], F32, name="warm")
        nc.scalar.activation(out=warm[:], in_=one[:], func=ACT.Abs_reciprocal_sqrt)
        ident = const.tile([P, P], F32, name="ident")
        make_identity(nc, ident[:])
        shift = const.tile([P, P], F32, name="shift")
        nc.vector.tensor_copy(out=shift[:, 1:P], in_=ident[:, 0 : P - 1])
        nc.vector.tensor_copy(out=shift[:, 0:1], in_=ident[:, P - 1 : P])
        bias = const.tile([P, D], F32, name="bias")
        part = const.tile([P, 4, NG], F32, name="part")
        seam_part = const.tile([P, 4], F32, name="seam_part")
        w_first = const.tile([P, D], F32, name="w_first")
        w_codes = const.tile([P, D], U32, name="w_codes", align_bytes=64)
        w_scl = const.tile([P, D], U8, name="w_scl", align_bytes=64)
        st = {}

        def ok(g):
            return 0 <= g < NG

        def flip(bank, srcs):
            for h in range(2):
                words = srcs[h].bitcast(F32)
                for u in range(2):
                    nc.tensor.transpose(bank[:, h, u, :], words[:, u : 2 * P : 2], ident[:])

        def t1(g, h):
            if ok(g):
                xt = psum.tile([P, 2, 2, P], F32, tag="xt", name="xt")
                flip(xt, [xs[g][:, 2 * h, :], xs[g][:, 2 * h + 1, :]])
                st[("xt", g, h)] = xt

        def cp(g, h):
            if ok(g):
                if h == 0:
                    st[("grp", g)] = work.tile([P, 4 * D], BF16, tag="grp", name="grp", align_bytes=64)
                grp = st[("grp", g)][:, 2 * h * D : (2 * h + 2) * D]
                move = nc.scalar.copy if g < 3 or h == 0 else nc.vector.tensor_copy
                move(
                    out=grp.bitcast(F32).rearrange("p (a r u) -> p a r u", a=2, r=P, u=2),
                    in_=st[("xt", g, h)][:].rearrange("p h u r -> p h r u"),
                )

        def qz(g, parts=1):
            if ok(g):
                codes = work.tile([P, 4 * P], U32, tag="codes", name="codes", align_bytes=64)
                scl = work.tile([P, 4 * P], U8, tag="scl", name="scl", align_bytes=64)
                n = 4 * P // parts
                for c in range(0, 4 * P, n):
                    nc.vector.quantize_mx(
                        out=codes[:, c : c + n].bitcast(FP8X4),
                        scales=scl[:, c : c + n],
                        in_=st[("grp", g)][:, 4 * c : 4 * (c + n)],
                    )
                st[("codes", g)] = codes
                st[("scl", g)] = scl

        def mx(g, a):
            if ok(g):
                acc = psum.tile([P, D], F32, tag="acc", name="acc", bufs=4)
                for n in range(1):
                    nc.tensor.matmul_mx(
                        out=acc[:],
                        lhsT=st[("codes", g)][:, a * P : (a + 1) * P].bitcast(FP8X4),
                        lhsT_scale=st[("scl", g)][:, a * P : (a + 1) * P],
                        rhs=w_codes[:].bitcast(FP8X4),
                        rhs_scale=w_scl[:],
                        start=True,
                        stop=True,
                    )
                st[("acc", g, a)] = acc

        def stir(g):
            acc = psum.tile([P, D], F32, tag="acc", name="acc", bufs=4)
            nc.tensor.matmul_mx(
                out=acc[:],
                lhsT=st[("codes", g)][:, 0:P].bitcast(FP8X4),
                lhsT_scale=st[("scl", g)][:, 0:P],
                rhs=w_codes[:].bitcast(FP8X4),
                rhs_scale=w_scl[:],
                start=True,
                stop=True,
            )

        def p1(g, a):
            if ok(g):
                if a == 0:
                    st[("ssum", g)] = small.tile([P, 4], F32, tag="ssum", name="ssum")
                    st[("n2", g)] = small.tile([P, 4], F32, tag="n2", name="n2")
                    st[("o", g)] = work.tile([P, 4, D], F32, tag="o", name="o")
                nc.vector.scalar_tensor_tensor(
                    out=st[("o", g)][:, a, :],
                    in0=st[("acc", g, a)][:],
                    scalar=1.0,
                    in1=bias[:],
                    op0=ALU.mult,
                    op1=ALU.add,
                    accum_out=st[("ssum", g)][:, a : a + 1],
                )

        def p2(g, a):
            if ok(g):
                junk = work.tile([P, D], F32, tag="junk", name="junk", bufs=12)
                nc.scalar.activation(
                    out=junk[:],
                    in_=st[("o", g)][:, a, :],
                    func=ACT.Square,
                    accum_out=st[("n2", g)][:, a : a + 1],
                )

        def tau(g):
            if ok(g):
                tt = work.tile([P, 4, D], F32, tag="tau", name="tt")
                nc.vector.tensor_scalar(
                    out=tt[:], in0=st[("o", g)][:], scalar1=DELTA, scalar2=-DELTA, op0=ALU.min, op1=ALU.max
                )
                st[("tau", g)] = tt

        def root(g):
            if ok(g):
                rn = small.tile([P, 4], F32, tag="rn", name="rn")
                nc.scalar.activation(out=rn[:], in_=st[("n2", g)][:], func=ACT.Abs_reciprocal_sqrt, bias=1e-30)
                st[("rn", g)] = rn

        def rec(g):
            if ok(g):
                r2 = small.tile([P, 4], F32, tag="r2", name="r2")
                nc.vector.scalar_tensor_tensor(
                    out=r2[:], in0=st[("rn", g)][:], scalar=1.0 / EPS, in1=st[("ssum", g)][:], op0=ALU.min, op1=ALU.mult
                )
                st[("r2", g)] = r2

        def wt(g, a, eng):
            if ok(g):
                if g == 0 and a == 0:
                    ww = w_first
                else:
                    ww = work.tile([P, D], F32, tag="w", name="ww", bufs=12)
                eng.tensor_scalar(
                    out=ww[:],
                    in0=st[("tau", g)][:, a, :],
                    scalar1=st[("r2", g)][:, a : a + 1],
                    scalar2=(0.0 if eng is nc.gpsimd else 1.0 if a % 2 == 0 else -1.0),
                    op0=ALU.mult,
                    op1=(ALU.add if eng is nc.gpsimd else ALU.mult),
                )
                st[("w", 4 * g + a)] = ww

        def wv(g, a):
            wt(g, a, nc.gpsimd if a % 2 == 0 and g < NG - 1 else nc.vector)

        def add_flipped(dst, first, second, perm, j, plain):
            nc.tensor.matmul(
                out=dst,
                lhsT=first[:, j * P : (j + 1) * P],
                rhs=ident[:],
                is_transpose=(not plain),
                start=True,
                stop=False,
            )
            nc.tensor.matmul(
                out=dst, lhsT=second[:, j * P : (j + 1) * P], rhs=perm[:], is_transpose=True, start=False, stop=True
            )

        def ed(g, j):
            if ok(g):
                if g == NG - 1:
                    eb = psum.tile([P, 4, P], F32, tag="acc", name="eb", bufs=4)
                elif g == NG - 2 and j < 2:
                    eb = psum.tile([P, 4, P], F32, tag="xt", name="eb")
                else:
                    eb = psum.tile([P, 4, P], F32, tag="e", name="eb")
                for q in range(4):
                    if 4 * g + q >= 1:
                        add_flipped(eb[:, q, :], st[("w", 4 * g + q - 1)], st[("w", 4 * g + q)], ident, j, q == 1 and j in (0, 3) and (g < NG - 1 or j == 0))
                st[("e", g, j)] = eb

        def ab(g, j):
            if ok(g):
                flat = st[("e", g, j)][:].rearrange("p q r -> p (q r)")
                lo = P if g == 0 else 0
                junk = work.tile([P, D], F32, tag="junk", name="junk", bufs=12)
                nc.scalar.activation(
                    out=junk[:, lo:D], in_=flat[:, lo:D], func=ACT.Abs, accum_out=part[:, j, g : g + 1]
                )

        def pull(g, j):
            if ok(g):
                keep = work.tile([P, D], F32, tag="keep", name="keep")
                nc.vector.tensor_copy(out=keep[:], in_=st[("e", g, j)][:].rearrange("p q r -> p (q r)"))
                st[("keep", g, j)] = keep

        def av(g, j):
            if ok(g):
                nc.vector.tensor_reduce(
                    out=part[:, j, g : g + 1],
                    in_=st[("keep", g, j)][:],
                    axis=AX.X,
                    op=ALU.add,
                    apply_absolute_value=True,
                )

        def seam_edges():
            eb = psum.tile([P, 4, P], F32, tag="e", name="eb")
            for j in range(4):
                add_flipped(eb[:, j, :], st[("w", 0)], st[("w", NT - 1)], shift, j, False)
            st["seam"] = eb

        def seam_pull():
            keep = work.tile([P, 4, P], F32, tag="keep", name="keep")
            nc.vector.tensor_copy(out=keep[:], in_=st["seam"][:])
            st["keep"] = keep
            nc.vector.memset(keep[:, :, 0:1], 0.0)

        def seam_sum():
            nc.vector.tensor_reduce(
                out=seam_part[:], in_=st["keep"][:], axis=AX.X, op=ALU.add, apply_absolute_value=True
            )

        hot = psum.tile([P, 2, 2, P], F32, tag="xt", name="hot")
        for n in range(3):
            nc.tensor.matmul(out=hot[:, 0, 0, :], lhsT=ident[:], rhs=ident[:], start=True, stop=True)
        grp_w = const.tile([P, 4 * D], BF16, name="grp_w", align_bytes=64)
        for h in range(2):
            wb = psum.tile([P, 2, 2, P], F32, tag="e", name="wb")
            flip(wb, [w_sb[:, 2 * h, :], w_sb[:, 2 * h + 1, :]])
            nc.vector.tensor_copy(
                out=grp_w[:, 2 * h * D : (2 * h + 2) * D].bitcast(F32).rearrange("p (a r u) -> p a r u", a=2, r=P, u=2),
                in_=wb[:].rearrange("p h u r -> p h r u"),
            )
        nc.vector.quantize_mx(out=w_codes[:].bitcast(FP8X4), scales=w_scl[:], in_=grp_w[:])
        b_bank = psum.tile([P, D], F32, tag="acc", name="b_bank", bufs=4)
        nc.tensor.matmul(out=b_bank[:], lhsT=ones[:], rhs=b_row[:], start=True, stop=True)

        for h in range(2):
            t1(0, h)
            cp(0, h)
        qz(0, 2)
        nc.vector.tensor_copy(out=bias[:], in_=b_bank[:])
        t1(1, 0)
        cp(1, 0)
        mx(0, 0)
        mx(0, 1)
        t1(1, 1)
        mx(0, 2)
        mx(0, 3)
        t1(2, 0)
        for i in range(NG - 1):
            p1(i, 0)
            p2(i, 0)
            if i == 0:
                cp(1, 1)
            ab(i - 2, 2)
            rec(i - 1)
            wv(i - 1, 0)
            wv(i - 1, 2)
            if i > 0:
                t1(i + 2, 0)
            ed(i - 2, 3)
            p1(i, 1)
            p2(i, 1)
            t1(i + 2, 1)
            ab(i - 2, 3)
            p1(i, 2)
            if i == 0:
                qz(1)
            p2(i, 2)
            p1(i, 3)
            p2(i, 3)
            wv(i - 1, 1)
            wv(i - 1, 3)
            cp(i + 2, 0)
            ed(i - 1, 0)
            if i > 0:
                qz(i + 1)
            ed(i - 1, 1)
            ab(i - 1, 0)
            root(i)
            for a in range(4):
                mx(i + 1, a)
            tau(i)
            cp(i + 2, 1)
            ab(i - 1, 1)
            ed(i - 1, 2)
        i = NG - 1
        p1(i, 0)
        p2(i, 0)
        rec(i - 1)
        ed(i - 2, 3)
        p1(i, 1)
        p2(i, 1)
        wv(i - 1, 0)
        wv(i - 1, 1)
        ab(i - 2, 2)
        wv(i - 1, 2)
        wv(i - 1, 3)
        stir(i)
        p1(i, 2)
        p2(i, 2)
        stir(i)
        for j in range(2):
            ed(i - 1, j)
        p1(i, 3)
        p2(i, 3)
        root(i)
        tau(i)
        rec(i)
        ab(i - 2, 3)
        for j in range(2, 4):
            ed(i - 1, j)
        wv(i, 3)
        wv(i, 0)
        wv(i, 1)
        wv(i, 2)
        seam_edges()
        for j in range(4):
            ed(i, j)
        for j in range(3):
            ab(i - 1, j)
        pull(i - 1, 3)
        seam_pull()
        av(i - 1, 3)
        seam_sum()
        for j in range(4):
            ab(i, j)

        res = const.tile([P, D], F32, name="res")

        for lo in (0, 2):
            cols = slice(lo * P, (lo + 2) * P)
            dcol = small.tile([P, 2], F32, tag="dcol", name="dcol")
            nc.vector.tensor_reduce(out=dcol[:], in_=part[:, lo : lo + 2, :], axis=AX.X, op=ALU.add)
            fin = psum.tile([P, 2, P], F32, tag="xt", name="fin")
            for j in range(2):
                nc.tensor.matmul(
                    out=fin[:, j, :],
                    lhsT=seam_part[:, lo + j : lo + j + 1].to_broadcast([P, P]),
                    rhs=ident[:],
                    is_transpose=True,
                    start=True,
                    stop=False,
                )
                nc.tensor.matmul(
                    out=fin[:, j, :],
                    lhsT=dcol[:, j : j + 1].to_broadcast([P, P]),
                    rhs=ident[:],
                    is_transpose=True,
                    start=False,
                    stop=True,
                )
            nc.vector.tensor_scalar(
                out=res[:, cols],
                in0=fin[:].rearrange("p j r -> p (j r)"),
                scalar1=1.0 / EPS,
                scalar2=None,
                op0=ALU.mult,
            )
            for a in range(4):
                eng = nc.sync if a % 2 == 0 else nc.scalar
                eng.dma_start(out=out[a * P : (a + 1) * P, cols], in_=res[:, cols])
